import numpy as np
import ml_dtypes

BF16 = ml_dtypes.bfloat16


def bf(x):
    return np.asarray(x, np.float32).astype(BF16)


def f32(x):
    return np.asarray(x, np.float32)


def f64(x):
    return np.asarray(x).astype(np.float64)


def striped(idx):
    return np.tile(idx.reshape(-1, 16).T, (8, 1))


D, S, M, N = 128, 1024, 512, 1024


def setup_inputs():
    return {"q": bf(np.random.standard_normal((D, S))), "k": bf(np.random.standard_normal((D, M))), "v": bf(2.0 * np.random.standard_normal((M, D))), "offs": striped(np.random.permutation(S)[:N])}


def reference(q, k, v, offs):
    idx = offs[:16].T.reshape(-1)
    logits = (f64(k).T @ f64(q)[:, idx]) / np.sqrt(D)
    e = np.exp(logits)
    return (f64(v).T @ e) / e.sum(axis=0, keepdims=True)

@@ -1,0 +1,134 @@
+import math
+
+import concourse.mybir as mybir
+from concourse.masks import make_identity
+
+BF16, F32, U16 = mybir.dt.bfloat16, mybir.dt.float32, mybir.dt.uint16
+EXP = mybir.ActivationFunctionType.Exp
+COPY = mybir.ActivationFunctionType.Copy
+X = mybir.AxisListType.X
+
+P = 128
+TOKENS = 1024
+KEYS = 512
+N = 1024
+PIECE = 512
+PIECES = N // PIECE
+KEY_BLOCKS = KEYS // P
+QUERY_BLOCKS = PIECE // P
+HALF = PIECE // 2
+ONES = P
+VALUE_COLUMNS = 144
+WARM_UPS = 4
+
+FLOPS = 2 * (2 * P * KEYS * N)
+
+
+def tile_longcontextattention_kernel(tc, q, k, v, offs, out):
+    nc = tc.nc
+    with (
+        tc.tile_pool(name="held", bufs=1) as held,
+        tc.tile_pool(name="work", bufs=2) as work,
+        tc.psum_pool(name="banks", bufs=8) as banks,
+    ):
+        offsets = held.tile([P, N // 16], U16, name="offsets")
+        nc.sync.dma_start(offsets[:], offs)
+        queries = held.tile([P, TOKENS], BF16, name="queries")
+        nc.scalar.dma_start(queries[:], q)
+        keys = held.tile([P, KEYS], BF16, name="keys")
+        nc.sync.dma_start(keys[:], k)
+
+        warm = held.tile([P, 1], F32, name="warm")
+        nc.vector.memset(warm[:], 0.0)
+        nc.scalar.activation(warm[:], warm[:], EXP)
+
+        values = held.tile([P, KEY_BLOCKS, VALUE_COLUMNS], BF16, name="values")
+        nc.gpsimd.dma_start(values[:, :, 0:P], v.rearrange("(b p) d -> p b d", p=P))
+        nc.vector.memset(values[:, :, ONES:VALUE_COLUMNS], 1.0)
+
+        identity = held.tile([P, P], F32, name="identity")
+        make_identity(nc, identity[:])
+        identity_bf16 = held.tile([P, P], BF16, name="identity_bf16")
+        make_identity(nc, identity_bf16[:])
+
+        zeros = held.tile([P, PIECE], BF16, name="zeros")
+        nc.vector.memset(zeros[:], 0.0)
+        for i in range(WARM_UPS):
+            unused = banks.tile([P, PIECE], F32, name="unused", tag="bank")
+            nc.tensor.matmul(unused[:], zeros[:, 0:P], zeros[:], start=True, stop=True)
+
+        logits = [[] for piece in range(PIECES)]
+        largest = [held.tile([P, PIECE], BF16, name=f"largest_{piece}") for piece in range(PIECES)]
+        for piece in range(PIECES):
+            piece_offsets = offsets[:, piece * (PIECE // 16) : (piece + 1) * (PIECE // 16)]
+            for b in range(KEY_BLOCKS):
+                product = banks.tile([P, PIECE], F32, name="product", tag="bank")
+                nc.tensor.matmul(
+                    product[:], keys[:, b * P : (b + 1) * P], queries[:].indirect(piece_offsets), start=True, stop=True
+                )
+                if b > 0:
+                    so_far = logits[piece][0] if b == 1 else largest[piece]
+                    nc.vector.tensor_max(largest[piece][:], product[:], so_far[:])
+                logits[piece].append(held.tile([P, PIECE], F32, name=f"logits_{piece}_{b}"))
+                nc.scalar.copy(logits[piece][b][:], product[:])
+
+        top = []
+        for piece in range(PIECES):
+            flipped_largest = banks.tile([P, QUERY_BLOCKS, P], BF16, name="flipped_largest", tag="bank")
+            for c in range(QUERY_BLOCKS):
+                nc.tensor.transpose(flipped_largest[:, c, :], largest[piece][:, c * P : (c + 1) * P], identity_bf16[:])
+            top.append(held.tile([P, QUERY_BLOCKS], BF16, name=f"top_{piece}"))
+            with nc.allow_low_precision(reason="the maximum of bfloat16 numbers is one of them"):
+                nc.vector.reduce_max(top[piece][:], flipped_largest[:], X)
+
+        tops = []
+        for piece in range(PIECES):
+            tops.append(banks.tile([P, PIECE], BF16, name=f"tops_{piece}", tag="bank"))
+            for c in range(QUERY_BLOCKS):
+                nc.tensor.transpose(
+                    tops[piece][:, c * P : (c + 1) * P], top[piece][:, c : c + 1].to_broadcast([P, P]), identity_bf16[:]
+                )
+
+        e = [[] for piece in range(PIECES)]
+        for piece in range(PIECES):
+            for b in range(KEY_BLOCKS):
+                shifted = held.tile([P, PIECE], F32, name=f"shifted_{piece}_{b}")
+                nc.vector.tensor_sub(shifted[:], logits[piece][b][:], tops[piece][:])
+                e[piece].append(held.tile([P, PIECE], BF16, name=f"e_{piece}_{b}"))
+                nc.scalar.activation(e[piece][b][:], shifted[:], EXP, scale=1.0 / math.sqrt(P))
+
+        sums = []
+        for piece in range(PIECES):
+            sums.append([banks.tile([P, P + 1], F32, name=f"sums_{piece}_{c}", tag="bank") for c in range(QUERY_BLOCKS)])
+            for b in range(KEY_BLOCKS):
+                for c in range(QUERY_BLOCKS):
+                    nc.tensor.matmul(
+                        sums[piece][c][:],
+                        e[piece][b][:, c * P : (c + 1) * P],
+                        values[:, b, 0 : P + 1],
+                        start=(b == 0),
+                        stop=(b == KEY_BLOCKS - 1),
+                    )
+
+        flipped = []
+        for piece in range(PIECES):
+            inverse = work.tile([P, QUERY_BLOCKS], F32, name="inverse")
+            for c in range(QUERY_BLOCKS):
+                nc.vector.reciprocal(inverse[:, c : c + 1], sums[piece][c][:, ONES : ONES + 1])
+            flipped.append([banks.tile([P, HALF], F32, name=f"flipped_{piece}_{h}", tag="bank") for h in range(2)])
+            for c in range(QUERY_BLOCKS):
+                attended = work.tile([P, P], F32, name="attended")
+                if c % 2 == 0:
+                    nc.vector.tensor_scalar_mul(attended[:], sums[piece][c][:, 0:P], inverse[:, c : c + 1])
+                else:
+                    nc.scalar.activation(attended[:], sums[piece][c][:, 0:P], COPY, scale=inverse[:, c : c + 1])
+                h, place = divmod(c * P, HALF)
+                nc.tensor.transpose(flipped[piece][h][:, place : place + P], attended[:], identity[:])
+
+        for piece in range(PIECES):
+            first = work.tile([P, HALF], F32, name="first")
+            nc.vector.tensor_copy(first[:], flipped[piece][0][:])
+            nc.sync.dma_start(out[:, piece * PIECE : piece * PIECE + HALF], first[:])
+            second = work.tile([P, HALF], F32, name="second")
+            nc.scalar.copy(second[:], flipped[piece][1][:])
+            nc.scalar.dma_start(out[:, piece * PIECE + HALF : (piece + 1) * PIECE], second[:])

@@ -5,20 +5,19 @@ from concourse.masks import make_identity
 
 BF16, F32, U16 = mybir.dt.bfloat16, mybir.dt.float32, mybir.dt.uint16
 EXP = mybir.ActivationFunctionType.Exp
-COPY = mybir.ActivationFunctionType.Copy
 X = mybir.AxisListType.X
 
 P = 128
 TOKENS = 1024
 KEYS = 512
 N = 1024
-PIECE = 512
-PIECES = N // PIECE
+BANK = 512
 KEY_BLOCKS = KEYS // P
-QUERY_BLOCKS = PIECE // P
-HALF = PIECE // 2
 ONES = P
 VALUE_COLUMNS = 144
+PIECE_WIDTHS = (384, 384, 256)
+PIECE_STARTS = (0, 384, 768)
+PIECES = len(PIECE_WIDTHS)
 WARM_UPS = 4
 
 FLOPS = 2 * (2 * P * KEYS * N)
@@ -51,84 +50,78 @@ def tile_longcontextattention_kernel(tc, q, k, v, offs, out):
         identity_bf16 = held.tile([P, P], BF16, name="identity_bf16")
         make_identity(nc, identity_bf16[:])
 
-        zeros = held.tile([P, PIECE], BF16, name="zeros")
+        zeros = held.tile([P, BANK], BF16, name="zeros")
         nc.vector.memset(zeros[:], 0.0)
         for i in range(WARM_UPS):
-            unused = banks.tile([P, PIECE], F32, name="unused", tag="bank")
+            unused = banks.tile([P, BANK], F32, name="unused", tag="bank")
             nc.tensor.matmul(unused[:], zeros[:, 0:P], zeros[:], start=True, stop=True)
 
         logits = [[] for piece in range(PIECES)]
-        largest = [held.tile([P, PIECE], BF16, name=f"largest_{piece}") for piece in range(PIECES)]
-        for piece in range(PIECES):
-            piece_offsets = offsets[:, piece * (PIECE // 16) : (piece + 1) * (PIECE // 16)]
+        largest = [held.tile([P, width], BF16, name=f"largest_{piece}") for piece, width in enumerate(PIECE_WIDTHS)]
+        for piece, (first, width) in enumerate(zip(PIECE_STARTS, PIECE_WIDTHS)):
+            piece_offsets = offsets[:, first // 16 : (first + width) // 16]
             for b in range(KEY_BLOCKS):
-                product = banks.tile([P, PIECE], F32, name="product", tag="bank")
+                product = banks.tile([P, width], F32, name="product", tag="bank")
                 nc.tensor.matmul(
                     product[:], keys[:, b * P : (b + 1) * P], queries[:].indirect(piece_offsets), start=True, stop=True
                 )
                 if b > 0:
                     so_far = logits[piece][0] if b == 1 else largest[piece]
                     nc.vector.tensor_max(largest[piece][:], product[:], so_far[:])
-                logits[piece].append(held.tile([P, PIECE], F32, name=f"logits_{piece}_{b}"))
+                logits[piece].append(held.tile([P, width], F32, name=f"logits_{piece}_{b}"))
                 nc.scalar.copy(logits[piece][b][:], product[:])
 
         top = []
-        for piece in range(PIECES):
-            flipped_largest = banks.tile([P, QUERY_BLOCKS, P], BF16, name="flipped_largest", tag="bank")
-            for c in range(QUERY_BLOCKS):
+        for piece, width in enumerate(PIECE_WIDTHS):
+            flipped_largest = banks.tile([P, width // P, P], BF16, name="flipped_largest", tag="bank")
+            for c in range(width // P):
                 nc.tensor.transpose(flipped_largest[:, c, :], largest[piece][:, c * P : (c + 1) * P], identity_bf16[:])
-            top.append(held.tile([P, QUERY_BLOCKS], BF16, name=f"top_{piece}"))
+            top.append(held.tile([P, width // P], BF16, name=f"top_{piece}"))
             with nc.allow_low_precision(reason="the maximum of bfloat16 numbers is one of them"):
                 nc.vector.reduce_max(top[piece][:], flipped_largest[:], X)
 
         tops = []
-        for piece in range(PIECES):
-            tops.append(banks.tile([P, PIECE], BF16, name=f"tops_{piece}", tag="bank"))
-            for c in range(QUERY_BLOCKS):
+        for piece, width in enumerate(PIECE_WIDTHS):
+            tops.append(banks.tile([P, width], BF16, name=f"tops_{piece}", tag="bank"))
+            for c in range(width // P):
                 nc.tensor.transpose(
                     tops[piece][:, c * P : (c + 1) * P], top[piece][:, c : c + 1].to_broadcast([P, P]), identity_bf16[:]
                 )
 
         e = [[] for piece in range(PIECES)]
-        for piece in range(PIECES):
+        for piece, width in enumerate(PIECE_WIDTHS):
             for b in range(KEY_BLOCKS):
-                shifted = held.tile([P, PIECE], F32, name=f"shifted_{piece}_{b}")
+                shifted = held.tile([P, width], F32, name=f"shifted_{piece}_{b}")
                 nc.vector.tensor_sub(shifted[:], logits[piece][b][:], tops[piece][:])
-                e[piece].append(held.tile([P, PIECE], BF16, name=f"e_{piece}_{b}"))
+                e[piece].append(held.tile([P, width], BF16, name=f"e_{piece}_{b}"))
                 nc.scalar.activation(e[piece][b][:], shifted[:], EXP, scale=1.0 / math.sqrt(P))
 
         sums = []
-        for piece in range(PIECES):
-            sums.append([banks.tile([P, P + 1], F32, name=f"sums_{piece}_{c}", tag="bank") for c in range(QUERY_BLOCKS)])
+        for piece, width in enumerate(PIECE_WIDTHS):
+            query_blocks = width // P
+            sums.append(banks.tile([P, query_blocks, P + 1], F32, name=f"sums_{piece}", tag="bank"))
             for b in range(KEY_BLOCKS):
-                for c in range(QUERY_BLOCKS):
+                for c in range(query_blocks):
                     nc.tensor.matmul(
-                        sums[piece][c][:],
+                        sums[piece][:, c, :],
                         e[piece][b][:, c * P : (c + 1) * P],
                         values[:, b, 0 : P + 1],
-                        start=(b == 0),
-                        stop=(b == KEY_BLOCKS - 1),
+                        start=(b == 0 and c == 0),
+                        stop=(b == KEY_BLOCKS - 1 and c == query_blocks - 1),
                     )
 
         flipped = []
-        for piece in range(PIECES):
-            inverse = work.tile([P, QUERY_BLOCKS], F32, name="inverse")
-            for c in range(QUERY_BLOCKS):
-                nc.vector.reciprocal(inverse[:, c : c + 1], sums[piece][c][:, ONES : ONES + 1])
-            flipped.append([banks.tile([P, HALF], F32, name=f"flipped_{piece}_{h}", tag="bank") for h in range(2)])
-            for c in range(QUERY_BLOCKS):
-                attended = work.tile([P, P], F32, name="attended")
-                if c % 2 == 0:
-                    nc.vector.tensor_scalar_mul(attended[:], sums[piece][c][:, 0:P], inverse[:, c : c + 1])
-                else:
-                    nc.scalar.activation(attended[:], sums[piece][c][:, 0:P], COPY, scale=inverse[:, c : c + 1])
-                h, place = divmod(c * P, HALF)
-                nc.tensor.transpose(flipped[piece][h][:, place : place + P], attended[:], identity[:])
+        for piece, width in enumerate(PIECE_WIDTHS):
+            query_blocks = width // P
+            inverse = work.tile([P, query_blocks, 1], F32, name="inverse")
+            nc.vector.reciprocal(inverse[:], sums[piece][:, :, ONES : ONES + 1])
+            attended = work.tile([P, query_blocks, P], F32, name="attended")
+            nc.vector.tensor_mul(attended[:], sums[piece][:, :, 0:P], inverse[:].to_broadcast([P, query_blocks, P]))
+            flipped.append(banks.tile([P, width], F32, name=f"flipped_{piece}", tag="bank"))
+            for c in range(query_blocks):
+                nc.tensor.transpose(flipped[piece][:, c * P : (c + 1) * P], attended[:, c, :], identity[:])
 
-        for piece in range(PIECES):
-            first = work.tile([P, HALF], F32, name="first")
-            nc.vector.tensor_copy(first[:], flipped[piece][0][:])
-            nc.sync.dma_start(out[:, piece * PIECE : piece * PIECE + HALF], first[:])
-            second = work.tile([P, HALF], F32, name="second")
-            nc.scalar.copy(second[:], flipped[piece][1][:])
-            nc.scalar.dma_start(out[:, piece * PIECE + HALF : (piece + 1) * PIECE], second[:])
+        for piece, (first, width) in enumerate(zip(PIECE_STARTS, PIECE_WIDTHS)):
+            result = held.tile([P, width], F32, name=f"result_{piece}")
+            nc.scalar.copy(result[:], flipped[piece][:])
+            nc.sync.dma_start(out[:, first : first + width], result[:])

@@ -18,7 +18,7 @@ VALUE_COLUMNS = 144
 PIECE_WIDTHS = (384, 384, 256)
 PIECE_STARTS = (0, 384, 768)
 PIECES = len(PIECE_WIDTHS)
-WARM_UPS = 4
+WARM_UPS = 3
 
 FLOPS = 2 * (2 * P * KEYS * N)
 
@@ -30,6 +30,12 @@ def tile_longcontextattention_kernel(tc, q, k, v, offs, out):
         tc.tile_pool(name="work", bufs=2) as work,
         tc.psum_pool(name="banks", bufs=8) as banks,
     ):
+        zeros = held.tile([P, BANK], BF16, name="zeros")
+        nc.vector.memset(zeros[:], 0.0)
+        for i in range(WARM_UPS):
+            unused = banks.tile([P, BANK], F32, name="unused", tag="bank")
+            nc.tensor.matmul(unused[:], zeros[:, 0:P], zeros[:], start=True, stop=True)
+
         offsets = held.tile([P, N // 16], U16, name="offsets")
         nc.sync.dma_start(offsets[:], offs)
         queries = held.tile([P, TOKENS], BF16, name="queries")
@@ -50,20 +56,17 @@ def tile_longcontextattention_kernel(tc, q, k, v, offs, out):
         identity_bf16 = held.tile([P, P], BF16, name="identity_bf16")
         make_identity(nc, identity_bf16[:])
 
-        zeros = held.tile([P, BANK], BF16, name="zeros")
-        nc.vector.memset(zeros[:], 0.0)
-        for i in range(WARM_UPS):
-            unused = banks.tile([P, BANK], F32, name="unused", tag="bank")
-            nc.tensor.matmul(unused[:], zeros[:, 0:P], zeros[:], start=True, stop=True)
-
         logits = [[] for piece in range(PIECES)]
         largest = [held.tile([P, width], BF16, name=f"largest_{piece}") for piece, width in enumerate(PIECE_WIDTHS)]
-        for piece, (first, width) in enumerate(zip(PIECE_STARTS, PIECE_WIDTHS)):
-            piece_offsets = offsets[:, first // 16 : (first + width) // 16]
-            for b in range(KEY_BLOCKS):
+        for b in range(KEY_BLOCKS):
+            for piece, (first, width) in enumerate(zip(PIECE_STARTS, PIECE_WIDTHS)):
                 product = banks.tile([P, width], F32, name="product", tag="bank")
                 nc.tensor.matmul(
-                    product[:], keys[:, b * P : (b + 1) * P], queries[:].indirect(piece_offsets), start=True, stop=True
+                    product[:],
+                    keys[:, b * P : (b + 1) * P],
+                    queries[:].indirect(offsets[:, first // 16 : (first + width) // 16]),
+                    start=True,
+                    stop=True,
                 )
                 if b > 0:
                     so_far = logits[piece][0] if b == 1 else largest[piece]

@@ -15,8 +15,8 @@ BANK = 512
 KEY_BLOCKS = KEYS // P
 ONES = P
 VALUE_COLUMNS = 144
-PIECE_WIDTHS = (384, 384, 256)
-PIECE_STARTS = (0, 384, 768)
+PIECE_WIDTHS = (256, 256, 256, 256)
+PIECE_STARTS = (0, 256, 512, 768)
 PIECES = len(PIECE_WIDTHS)
 WARM_UPS = 3
 

@@ -56,7 +56,7 @@ def tile_longcontextattention_kernel(tc, q, k, v, offs, out):
         identity_bf16 = held.tile([P, P], BF16, name="identity_bf16")
         make_identity(nc, identity_bf16[:])
 
-        logits = [[] for piece in range(PIECES)]
+        logits = [held.tile([P, KEY_BLOCKS, width], F32, name=f"logits_{piece}") for piece, width in enumerate(PIECE_WIDTHS)]
         largest = [held.tile([P, width], BF16, name=f"largest_{piece}") for piece, width in enumerate(PIECE_WIDTHS)]
         for b in range(KEY_BLOCKS):
             for piece, (first, width) in enumerate(zip(PIECE_STARTS, PIECE_WIDTHS)):
@@ -69,10 +69,9 @@ def tile_longcontextattention_kernel(tc, q, k, v, offs, out):
                     stop=True,
                 )
                 if b > 0:
-                    so_far = logits[piece][0] if b == 1 else largest[piece]
-                    nc.vector.tensor_max(largest[piece][:], product[:], so_far[:])
-                logits[piece].append(held.tile([P, width], F32, name=f"logits_{piece}_{b}"))
-                nc.scalar.copy(logits[piece][b][:], product[:])
+                    so_far = logits[piece][:, 0, :] if b == 1 else largest[piece][:]
+                    nc.vector.tensor_max(largest[piece][:], product[:], so_far)
+                nc.scalar.copy(logits[piece][:, b, :], product[:])
 
         top = []
         for piece, width in enumerate(PIECE_WIDTHS):
@@ -91,13 +90,13 @@ def tile_longcontextattention_kernel(tc, q, k, v, offs, out):
                     tops[piece][:, c * P : (c + 1) * P], top[piece][:, c : c + 1].to_broadcast([P, P]), identity_bf16[:]
                 )
 
-        e = [[] for piece in range(PIECES)]
+        e = [held.tile([P, KEY_BLOCKS, width], BF16, name=f"e_{piece}") for piece, width in enumerate(PIECE_WIDTHS)]
         for piece, width in enumerate(PIECE_WIDTHS):
-            for b in range(KEY_BLOCKS):
-                shifted = held.tile([P, width], F32, name=f"shifted_{piece}_{b}")
-                nc.vector.tensor_sub(shifted[:], logits[piece][b][:], tops[piece][:])
-                e[piece].append(held.tile([P, width], BF16, name=f"e_{piece}_{b}"))
-                nc.scalar.activation(e[piece][b][:], shifted[:], EXP, scale=1.0 / math.sqrt(P))
+            for b in range(0, KEY_BLOCKS, 2):
+                shifted = held.tile([P, 2, width], F32, name=f"shifted_{piece}_{b}")
+                both = tops[piece][:].unsqueeze(1).to_broadcast([P, 2, width])
+                nc.vector.tensor_sub(shifted[:], logits[piece][:, b : b + 2, :], both)
+                nc.scalar.activation(e[piece][:, b : b + 2, :], shifted[:], EXP, scale=1.0 / math.sqrt(P))
 
         sums = []
         for piece, width in enumerate(PIECE_WIDTHS):
@@ -107,7 +106,7 @@ def tile_longcontextattention_kernel(tc, q, k, v, offs, out):
                 for c in range(query_blocks):
                     nc.tensor.matmul(
                         sums[piece][:, c, :],
-                        e[piece][b][:, c * P : (c + 1) * P],
+                        e[piece][:, b, c * P : (c + 1) * P],
                         values[:, b, 0 : P + 1],
                         start=(b == 0 and c == 0),
                         stop=(b == KEY_BLOCKS - 1 and c == query_blocks - 1),

@@ -112,18 +112,19 @@ def tile_longcontextattention_kernel(tc, q, k, v, offs, out):
                         stop=(b == KEY_BLOCKS - 1 and c == query_blocks - 1),
                     )
 
-        flipped = []
+        flipped = [[] for piece in range(PIECES)]
         for piece, width in enumerate(PIECE_WIDTHS):
             query_blocks = width // P
             inverse = work.tile([P, query_blocks, 1], F32, name="inverse")
             nc.vector.reciprocal(inverse[:], sums[piece][:, :, ONES : ONES + 1])
-            attended = work.tile([P, query_blocks, P], F32, name="attended")
-            nc.vector.tensor_mul(attended[:], sums[piece][:, :, 0:P], inverse[:].to_broadcast([P, query_blocks, P]))
-            flipped.append(banks.tile([P, width], F32, name=f"flipped_{piece}", tag="bank"))
             for c in range(query_blocks):
-                nc.tensor.transpose(flipped[piece][:, c * P : (c + 1) * P], attended[:, c, :], identity[:])
+                attended = held.tile([P, P], F32, name=f"attended_{piece}_{c}")
+                nc.vector.tensor_scalar_mul(attended[:], sums[piece][:, c, 0:P], inverse[:, c, :])
+                flipped[piece].append(banks.tile([P, P], F32, name=f"flipped_{piece}_{c}", tag="bank"))
+                nc.tensor.transpose(flipped[piece][c][:], attended[:], identity[:])
 
         for piece, (first, width) in enumerate(zip(PIECE_STARTS, PIECE_WIDTHS)):
-            result = held.tile([P, width], F32, name=f"result_{piece}")
-            nc.scalar.copy(result[:], flipped[piece][:])
-            nc.sync.dma_start(out[:, first : first + width], result[:])
+            for c in range(width // P):
+                result = held.tile([P, P], F32, name=f"result_{piece}_{c}")
+                nc.scalar.copy(result[:], flipped[piece][c][:])
+                nc.sync.dma_start(out[:, first + c * P : first + (c + 1) * P], result[:])

@@ -3,8 +3,9 @@ import math
 import concourse.mybir as mybir
 from concourse.masks import make_identity
 
-BF16, F32, U16 = mybir.dt.bfloat16, mybir.dt.float32, mybir.dt.uint16
+BF16, F32, U16, I32 = mybir.dt.bfloat16, mybir.dt.float32, mybir.dt.uint16, mybir.dt.int32
 EXP = mybir.ActivationFunctionType.Exp
+MULT, ADD = mybir.AluOpType.mult, mybir.AluOpType.add
 X = mybir.AxisListType.X
 
 P = 128
@@ -13,12 +14,19 @@ KEYS = 512
 N = 1024
 BANK = 512
 KEY_BLOCKS = KEYS // P
+WIDTH = 256
+PIECES = N // WIDTH
+EARLY, LATE = (0, 1), (2, 3)
+QUERY_BLOCKS = WIDTH // P
+HALVES = (slice(0, 2), slice(2, 4))
 ONES = P
 VALUE_COLUMNS = 144
-PIECE_WIDTHS = (256, 256, 256, 256)
-PIECE_STARTS = (0, 256, 512, 768)
-PIECES = len(PIECE_WIDTHS)
 WARM_UPS = 3
+
+SCALE = 1.0 / math.sqrt(P)
+TEMPERATURE = 9.0
+BIT_STEP = TEMPERATURE * math.log(2.0) / 2.0**23 / SCALE
+SHIFT_BIAS = TEMPERATURE * (127 * math.log(2.0) + 0.5 * math.log(KEYS))
 
 FLOPS = 2 * (2 * P * KEYS * N)
 
@@ -27,7 +35,6 @@ def tile_longcontextattention_kernel(tc, q, k, v, offs, out):
     nc = tc.nc
     with (
         tc.tile_pool(name="held", bufs=1) as held,
-        tc.tile_pool(name="work", bufs=2) as work,
         tc.psum_pool(name="banks", bufs=8) as banks,
     ):
         zeros = held.tile([P, BANK], BF16, name="zeros")
@@ -51,80 +58,139 @@ def tile_longcontextattention_kernel(tc, q, k, v, offs, out):
         nc.gpsimd.dma_start(values[:, :, 0:P], v.rearrange("(b p) d -> p b d", p=P))
         nc.vector.memset(values[:, :, ONES:VALUE_COLUMNS], 1.0)
 
+        all_ones = held.tile([P, P], BF16, name="all_ones")
+        nc.vector.memset(all_ones[:], 1.0)
+        shift_bias = held.tile([P, 1], F32, name="shift_bias")
+        nc.vector.memset(shift_bias[:], SHIFT_BIAS)
         identity = held.tile([P, P], F32, name="identity")
         make_identity(nc, identity[:])
         identity_bf16 = held.tile([P, P], BF16, name="identity_bf16")
         make_identity(nc, identity_bf16[:])
 
-        logits = [held.tile([P, KEY_BLOCKS, width], F32, name=f"logits_{piece}") for piece, width in enumerate(PIECE_WIDTHS)]
-        largest = [held.tile([P, width], BF16, name=f"largest_{piece}") for piece, width in enumerate(PIECE_WIDTHS)]
-        for b in range(KEY_BLOCKS):
-            for piece, (first, width) in enumerate(zip(PIECE_STARTS, PIECE_WIDTHS)):
-                product = banks.tile([P, width], F32, name="product", tag="bank")
-                nc.tensor.matmul(
-                    product[:],
-                    keys[:, b * P : (b + 1) * P],
-                    queries[:].indirect(offsets[:, first // 16 : (first + width) // 16]),
-                    start=True,
-                    stop=True,
-                )
-                if b > 0:
-                    so_far = logits[piece][:, 0, :] if b == 1 else largest[piece][:]
-                    nc.vector.tensor_max(largest[piece][:], product[:], so_far)
-                nc.scalar.copy(logits[piece][:, b, :], product[:])
+        def gathered_product(product, piece, block):
+            nc.tensor.matmul(
+                product,
+                keys[:, block * P : (block + 1) * P],
+                queries[:].indirect(offsets[:, piece * WIDTH // 16 : (piece + 1) * WIDTH // 16]),
+                start=True,
+                stop=True,
+            )
 
-        top = []
-        for piece, width in enumerate(PIECE_WIDTHS):
-            flipped_largest = banks.tile([P, width // P, P], BF16, name="flipped_largest", tag="bank")
-            for c in range(width // P):
+        logits = {}
+        for piece in EARLY:
+            for half in range(2):
+                logits[piece, half] = held.tile([P, 2, WIDTH], F32, name=f"logits_{piece}_{half}")
+        largest = {piece: held.tile([P, WIDTH], BF16, name=f"largest_{piece}") for piece in EARLY}
+        top = {}
+        tops = {}
+        rough = {}
+        mass = {}
+        e = {}
+        sums = {}
+
+        def early_product(piece, block):
+            product = banks.tile([P, WIDTH], F32, name="product", tag="bank")
+            gathered_product(product[:], piece, block)
+            if block > 0:
+                so_far = logits[piece, 0][:, 0, :] if block == 1 else largest[piece][:]
+                nc.vector.tensor_max(largest[piece][:], product[:], so_far)
+            nc.scalar.copy(logits[piece, block // 2][:, block % 2, :], product[:])
+
+        def largest_over_partitions(piece):
+            flipped_largest = banks.tile([P, QUERY_BLOCKS, P], BF16, name="flipped_largest", tag="bank")
+            for c in range(QUERY_BLOCKS):
                 nc.tensor.transpose(flipped_largest[:, c, :], largest[piece][:, c * P : (c + 1) * P], identity_bf16[:])
-            top.append(held.tile([P, width // P], BF16, name=f"top_{piece}"))
+            top[piece] = held.tile([P, QUERY_BLOCKS], BF16, name=f"top_{piece}")
             with nc.allow_low_precision(reason="the maximum of bfloat16 numbers is one of them"):
                 nc.vector.reduce_max(top[piece][:], flipped_largest[:], X)
 
-        tops = []
-        for piece, width in enumerate(PIECE_WIDTHS):
-            tops.append(banks.tile([P, width], BF16, name=f"tops_{piece}", tag="bank"))
-            for c in range(width // P):
+        def spread_tops(piece):
+            tops[piece] = banks.tile([P, WIDTH], BF16, name=f"tops_{piece}", tag="bank")
+            for c in range(QUERY_BLOCKS):
                 nc.tensor.transpose(
                     tops[piece][:, c * P : (c + 1) * P], top[piece][:, c : c + 1].to_broadcast([P, P]), identity_bf16[:]
                 )
 
-        e = [held.tile([P, KEY_BLOCKS, width], BF16, name=f"e_{piece}") for piece, width in enumerate(PIECE_WIDTHS)]
-        for piece, width in enumerate(PIECE_WIDTHS):
-            for b in range(0, KEY_BLOCKS, 2):
-                shifted = held.tile([P, 2, width], F32, name=f"shifted_{piece}_{b}")
-                both = tops[piece][:].unsqueeze(1).to_broadcast([P, 2, width])
-                nc.vector.tensor_sub(shifted[:], logits[piece][:, b : b + 2, :], both)
-                nc.scalar.activation(e[piece][:, b : b + 2, :], shifted[:], EXP, scale=1.0 / math.sqrt(P))
+        def late_products(piece, half):
+            logits[piece, half] = banks.tile([P, 2, WIDTH], F32, name=f"logits_{piece}_{half}", tag="bank")
+            for b in range(2):
+                gathered_product(logits[piece, half][:, b, :], piece, 2 * half + b)
 
-        sums = []
-        for piece, width in enumerate(PIECE_WIDTHS):
-            query_blocks = width // P
-            sums.append(banks.tile([P, query_blocks, P + 1], F32, name=f"sums_{piece}", tag="bank"))
+        def flatten(piece):
+            rough[piece] = held.tile([P, KEY_BLOCKS, WIDTH], BF16, name=f"rough_{piece}")
+            for half in range(2):
+                nc.scalar.activation(
+                    rough[piece][:, HALVES[half], :], logits[piece, half][:], EXP, scale=SCALE / TEMPERATURE
+                )
+
+        def weigh(piece):
+            mass_sum = banks.tile([P, WIDTH], F32, name="mass_sum", tag="bank")
             for b in range(KEY_BLOCKS):
-                for c in range(query_blocks):
+                nc.tensor.matmul(
+                    mass_sum[:], all_ones[:], rough[piece][:, b, :], start=(b == 0), stop=(b == KEY_BLOCKS - 1)
+                )
+            mass[piece] = held.tile([P, WIDTH], F32, name=f"mass_{piece}")
+            nc.vector.tensor_copy(mass[piece][:], mass_sum[:])
+
+        def exponentiate(piece):
+            e[piece] = held.tile([P, KEY_BLOCKS, WIDTH], BF16, name=f"e_{piece}")
+            for half in range(2):
+                shifted = held.tile([P, 2, WIDTH], F32, name=f"shifted_{piece}_{half}")
+                if piece in EARLY:
+                    both = tops[piece][:].unsqueeze(1).to_broadcast([P, 2, WIDTH])
+                    nc.vector.tensor_sub(shifted[:], logits[piece, half][:], both)
+                    nc.scalar.activation(e[piece][:, HALVES[half], :], shifted[:], EXP, scale=SCALE)
+                else:
+                    both = mass[piece][:].bitcast(I32).unsqueeze(1).to_broadcast([P, 2, WIDTH])
+                    nc.vector.scalar_tensor_tensor(shifted[:], both, -BIT_STEP, logits[piece, half][:], MULT, ADD)
+                    nc.scalar.activation(e[piece][:, HALVES[half], :], shifted[:], EXP, bias=shift_bias[:], scale=SCALE)
+
+        def attend(piece):
+            sums[piece] = banks.tile([P, QUERY_BLOCKS, P + 1], F32, name=f"sums_{piece}", tag="bank")
+            for b in range(KEY_BLOCKS):
+                for c in range(QUERY_BLOCKS):
                     nc.tensor.matmul(
                         sums[piece][:, c, :],
                         e[piece][:, b, c * P : (c + 1) * P],
                         values[:, b, 0 : P + 1],
                         start=(b == 0 and c == 0),
-                        stop=(b == KEY_BLOCKS - 1 and c == query_blocks - 1),
+                        stop=(b == KEY_BLOCKS - 1 and c == QUERY_BLOCKS - 1),
                     )
 
-        flipped = [[] for piece in range(PIECES)]
-        for piece, width in enumerate(PIECE_WIDTHS):
-            query_blocks = width // P
-            inverse = work.tile([P, query_blocks, 1], F32, name="inverse")
+        for block in range(KEY_BLOCKS):
+            for piece in EARLY:
+                early_product(piece, block)
+        late_products(LATE[0], 0)
+        for piece in EARLY:
+            largest_over_partitions(piece)
+        late_products(LATE[0], 1)
+        for piece in EARLY:
+            spread_tops(piece)
+        for half in range(2):
+            late_products(LATE[1], half)
+
+        for early, late in zip(EARLY, LATE):
+            flatten(late)
+            exponentiate(early)
+        for piece in LATE:
+            weigh(piece)
+            exponentiate(piece)
+        for piece in range(PIECES):
+            attend(piece)
+
+        flipped = {}
+        for piece in range(PIECES):
+            inverse = held.tile([P, QUERY_BLOCKS, 1], F32, name=f"inverse_{piece}")
             nc.vector.reciprocal(inverse[:], sums[piece][:, :, ONES : ONES + 1])
-            for c in range(query_blocks):
+            for c in range(QUERY_BLOCKS):
                 attended = held.tile([P, P], F32, name=f"attended_{piece}_{c}")
                 nc.vector.tensor_scalar_mul(attended[:], sums[piece][:, c, 0:P], inverse[:, c, :])
-                flipped[piece].append(banks.tile([P, P], F32, name=f"flipped_{piece}_{c}", tag="bank"))
-                nc.tensor.transpose(flipped[piece][c][:], attended[:], identity[:])
+                flipped[piece, c] = banks.tile([P, P], F32, name=f"flipped_{piece}_{c}", tag="bank")
+                nc.tensor.transpose(flipped[piece, c][:], attended[:], identity[:])
 
-        for piece, (first, width) in enumerate(zip(PIECE_STARTS, PIECE_WIDTHS)):
-            for c in range(width // P):
+        for piece in range(PIECES):
+            for c in range(QUERY_BLOCKS):
+                first = piece * WIDTH + c * P
                 result = held.tile([P, P], F32, name=f"result_{piece}_{c}")
-                nc.scalar.copy(result[:], flipped[piece][c][:])
-                nc.sync.dma_start(out[:, first + c * P : first + (c + 1) * P], result[:])
+                nc.scalar.copy(result[:], flipped[piece, c][:])
+                nc.sync.dma_start(out[:, first : first + P], result[:])

@@ -178,19 +178,20 @@ def tile_longcontextattention_kernel(tc, q, k, v, offs, out):
         for piece in range(PIECES):
             attend(piece)
 
-        flipped = {}
         for piece in range(PIECES):
             inverse = held.tile([P, QUERY_BLOCKS, 1], F32, name=f"inverse_{piece}")
             nc.vector.reciprocal(inverse[:], sums[piece][:, :, ONES : ONES + 1])
-            for c in range(QUERY_BLOCKS):
-                attended = held.tile([P, P], F32, name=f"attended_{piece}_{c}")
-                nc.vector.tensor_scalar_mul(attended[:], sums[piece][:, c, 0:P], inverse[:, c, :])
-                flipped[piece, c] = banks.tile([P, P], F32, name=f"flipped_{piece}_{c}", tag="bank")
-                nc.tensor.transpose(flipped[piece, c][:], attended[:], identity[:])
-
-        for piece in range(PIECES):
-            for c in range(QUERY_BLOCKS):
+            blocks_at_once = QUERY_BLOCKS if piece < PIECES - 1 else 1
+            for c in range(0, QUERY_BLOCKS, blocks_at_once):
+                these = slice(c, c + blocks_at_once)
+                shape = [P, blocks_at_once, P]
+                attended = held.tile(shape, F32, name=f"attended_{piece}_{c}")
+                nc.vector.tensor_mul(attended[:], sums[piece][:, these, 0:P], inverse[:, these, :].to_broadcast(shape))
+                flipped = banks.tile(shape, F32, name="flipped", tag="bank")
+                for b in range(blocks_at_once):
+                    nc.tensor.transpose(flipped[:, b, :], attended[:, b, :], identity[:])
+                result = held.tile(shape, F32, name=f"result_{piece}_{c}")
+                nc.scalar.copy(result[:], flipped[:])
                 first = piece * WIDTH + c * P
-                result = held.tile([P, P], F32, name=f"result_{piece}_{c}")
-                nc.scalar.copy(result[:], flipped[piece, c][:])
-                nc.sync.dma_start(out[:, first : first + P], result[:])
+                columns = out[:, first : first + blocks_at_once * P]
+                nc.sync.dma_start(columns.rearrange("d (b i) -> d b i", b=blocks_at_once), result[:])

@@ -111,10 +111,11 @@ def tile_longcontextattention_kernel(tc, q, k, v, offs, out):
                     tops[piece][:, c * P : (c + 1) * P], top[piece][:, c : c + 1].to_broadcast([P, P]), identity_bf16[:]
                 )
 
-        def late_products(piece, half):
-            logits[piece, half] = banks.tile([P, 2, WIDTH], F32, name=f"logits_{piece}_{half}", tag="bank")
-            for b in range(2):
-                gathered_product(logits[piece, half][:, b, :], piece, 2 * half + b)
+        def late_product(piece, block):
+            half = block // 2
+            if block % 2 == 0:
+                logits[piece, half] = banks.tile([P, 2, WIDTH], F32, name=f"logits_{piece}_{half}", tag="bank")
+            gathered_product(logits[piece, half][:, block % 2, :], piece, block)
 
         def flatten(piece):
             rough[piece] = held.tile([P, KEY_BLOCKS, WIDTH], BF16, name=f"rough_{piece}")
@@ -160,14 +161,16 @@ def tile_longcontextattention_kernel(tc, q, k, v, offs, out):
         for block in range(KEY_BLOCKS):
             for piece in EARLY:
                 early_product(piece, block)
-        late_products(LATE[0], 0)
-        for piece in EARLY:
-            largest_over_partitions(piece)
-        late_products(LATE[0], 1)
-        for piece in EARLY:
-            spread_tops(piece)
-        for half in range(2):
-            late_products(LATE[1], half)
+        late = [(piece, block) for piece in LATE for block in range(KEY_BLOCKS)]
+        issued = 0
+        for step in (largest_over_partitions, spread_tops):
+            for early_piece, products in zip(EARLY, (2, 1)):
+                for late_piece, block in late[issued : issued + products]:
+                    late_product(late_piece, block)
+                issued += products
+                step(early_piece)
+        for late_piece, block in late[issued:]:
+            late_product(late_piece, block)
 
         for early, late in zip(EARLY, LATE):
             flatten(late)

@@ -137,7 +137,11 @@ def tile_longcontextattention_kernel(tc, q, k, v, offs, out):
             e[piece] = held.tile([P, KEY_BLOCKS, WIDTH], BF16, name=f"e_{piece}")
             for half in range(2):
                 shifted = held.tile([P, 2, WIDTH], F32, name=f"shifted_{piece}_{half}")
-                if piece in EARLY:
+                if piece == EARLY[1] and half == 1:
+                    both = tops_copy[:].unsqueeze(1).to_broadcast([P, 2, WIDTH])
+                    nc.gpsimd.tensor_sub(shifted[:], logits[piece, half][:], both)
+                    nc.scalar.activation(e[piece][:, HALVES[half], :], shifted[:], EXP, scale=SCALE)
+                elif piece in EARLY:
                     both = tops[piece][:].unsqueeze(1).to_broadcast([P, 2, WIDTH])
                     nc.vector.tensor_sub(shifted[:], logits[piece, half][:], both)
                     nc.scalar.activation(e[piece][:, HALVES[half], :], shifted[:], EXP, scale=SCALE)
@@ -169,6 +173,8 @@ def tile_longcontextattention_kernel(tc, q, k, v, offs, out):
                     late_product(late_piece, block)
                 issued += products
                 step(early_piece)
+        tops_copy = held.tile([P, WIDTH], BF16, name="tops_copy")
+        nc.vector.tensor_copy(tops_copy[:], tops[EARLY[1]][:])
         for late_piece, block in late[issued:]:
             late_product(late_piece, block)
 

import math

import concourse.mybir as mybir
from concourse.masks import make_identity

BF16, F32, U16, I32 = mybir.dt.bfloat16, mybir.dt.float32, mybir.dt.uint16, mybir.dt.int32
EXP = mybir.ActivationFunctionType.Exp
MULT, ADD = mybir.AluOpType.mult, mybir.AluOpType.add
X = mybir.AxisListType.X

P = 128
TOKENS = 1024
KEYS = 512
N = 1024
BANK = 512
KEY_BLOCKS = KEYS // P
WIDTH = 256
PIECES = N // WIDTH
EARLY, LATE = (0, 1), (2, 3)
QUERY_BLOCKS = WIDTH // P
HALVES = (slice(0, 2), slice(2, 4))
ONES = P
VALUE_COLUMNS = 144
WARM_UPS = 3

SCALE = 1.0 / math.sqrt(P)
TEMPERATURE = 9.0
BIT_STEP = TEMPERATURE * math.log(2.0) / 2.0**23 / SCALE
SHIFT_BIAS = TEMPERATURE * (127 * math.log(2.0) + 0.5 * math.log(KEYS))

FLOPS = 2 * (2 * P * KEYS * N)


def tile_longcontextattention_kernel(tc, q, k, v, offs, out):
    nc = tc.nc
    with (
        tc.tile_pool(name="held", bufs=1) as held,
        tc.psum_pool(name="banks", bufs=8) as banks,
    ):
        zeros = held.tile([P, BANK], BF16, name="zeros")
        nc.vector.memset(zeros[:], 0.0)
        for i in range(WARM_UPS):
            unused = banks.tile([P, BANK], F32, name="unused", tag="bank")
            nc.tensor.matmul(unused[:], zeros[:, 0:P], zeros[:], start=True, stop=True)

        offsets = held.tile([P, N // 16], U16, name="offsets")
        nc.sync.dma_start(offsets[:], offs)
        queries = held.tile([P, TOKENS], BF16, name="queries")
        nc.scalar.dma_start(queries[:], q)
        keys = held.tile([P, KEYS], BF16, name="keys")
        nc.sync.dma_start(keys[:], k)

        warm = held.tile([P, 1], F32, name="warm")
        nc.vector.memset(warm[:], 0.0)
        nc.scalar.activation(warm[:], warm[:], EXP)

        values = held.tile([P, KEY_BLOCKS, VALUE_COLUMNS], BF16, name="values")
        nc.gpsimd.dma_start(values[:, :, 0:P], v.rearrange("(b p) d -> p b d", p=P))
        nc.vector.memset(values[:, :, ONES:VALUE_COLUMNS], 1.0)

        all_ones = held.tile([P, P], BF16, name="all_ones")
        nc.vector.memset(all_ones[:], 1.0)
        shift_bias = held.tile([P, 1], F32, name="shift_bias")
        nc.vector.memset(shift_bias[:], SHIFT_BIAS)
        identity = held.tile([P, P], F32, name="identity")
        make_identity(nc, identity[:])
        identity_bf16 = held.tile([P, P], BF16, name="identity_bf16")
        make_identity(nc, identity_bf16[:])

        def gathered_product(product, piece, block):
            nc.tensor.matmul(
                product,
                keys[:, block * P : (block + 1) * P],
                queries[:].indirect(offsets[:, piece * WIDTH // 16 : (piece + 1) * WIDTH // 16]),
                start=True,
                stop=True,
            )

        logits = {}
        for piece in EARLY:
            for half in range(2):
                logits[piece, half] = held.tile([P, 2, WIDTH], F32, name=f"logits_{piece}_{half}")
        largest = {piece: held.tile([P, WIDTH], BF16, name=f"largest_{piece}") for piece in EARLY}
        top = {}
        tops = {}
        rough = {}
        mass = {}
        e = {}
        sums = {}

        def early_product(piece, block):
            product = banks.tile([P, WIDTH], F32, name="product", tag="bank")
            gathered_product(product[:], piece, block)
            if block > 0:
                so_far = logits[piece, 0][:, 0, :] if block == 1 else largest[piece][:]
                nc.vector.tensor_max(largest[piece][:], product[:], so_far)
            nc.scalar.copy(logits[piece, block // 2][:, block % 2, :], product[:])

        def largest_over_partitions(piece):
            flipped_largest = banks.tile([P, QUERY_BLOCKS, P], BF16, name="flipped_largest", tag="bank")
            for c in range(QUERY_BLOCKS):
                nc.tensor.transpose(flipped_largest[:, c, :], largest[piece][:, c * P : (c + 1) * P], identity_bf16[:])
            top[piece] = held.tile([P, QUERY_BLOCKS], BF16, name=f"top_{piece}")
            with nc.allow_low_precision(reason="the maximum of bfloat16 numbers is one of them"):
                nc.vector.reduce_max(top[piece][:], flipped_largest[:], X)

        def spread_tops(piece):
            tops[piece] = banks.tile([P, WIDTH], BF16, name=f"tops_{piece}", tag="bank")
            for c in range(QUERY_BLOCKS):
                nc.tensor.transpose(
                    tops[piece][:, c * P : (c + 1) * P], top[piece][:, c : c + 1].to_broadcast([P, P]), identity_bf16[:]
                )

        def late_product(piece, block):
            half = block // 2
            if block % 2 == 0:
                logits[piece, half] = banks.tile([P, 2, WIDTH], F32, name=f"logits_{piece}_{half}", tag="bank")
            gathered_product(logits[piece, half][:, block % 2, :], piece, block)

        def flatten(piece):
            rough[piece] = held.tile([P, KEY_BLOCKS, WIDTH], BF16, name=f"rough_{piece}")
            for half in range(2):
                nc.scalar.activation(
                    rough[piece][:, HALVES[half], :], logits[piece, half][:], EXP, scale=SCALE / TEMPERATURE
                )

        def weigh(piece):
            mass_sum = banks.tile([P, WIDTH], F32, name="mass_sum", tag="bank")
            for b in range(KEY_BLOCKS):
                nc.tensor.matmul(
                    mass_sum[:], all_ones[:], rough[piece][:, b, :], start=(b == 0), stop=(b == KEY_BLOCKS - 1)
                )
            mass[piece] = held.tile([P, WIDTH], F32, name=f"mass_{piece}")
            nc.vector.tensor_copy(mass[piece][:], mass_sum[:])

        def exponentiate(piece):
            e[piece] = held.tile([P, KEY_BLOCKS, WIDTH], BF16, name=f"e_{piece}")
            for half in range(2):
                shifted = held.tile([P, 2, WIDTH], F32, name=f"shifted_{piece}_{half}")
                if piece == EARLY[1] and half == 1:
                    both = tops_copy[:].unsqueeze(1).to_broadcast([P, 2, WIDTH])
                    nc.gpsimd.tensor_sub(shifted[:], logits[piece, half][:], both)
                    nc.scalar.activation(e[piece][:, HALVES[half], :], shifted[:], EXP, scale=SCALE)
                elif piece in EARLY:
                    both = tops[piece][:].unsqueeze(1).to_broadcast([P, 2, WIDTH])
                    nc.vector.tensor_sub(shifted[:], logits[piece, half][:], both)
                    nc.scalar.activation(e[piece][:, HALVES[half], :], shifted[:], EXP, scale=SCALE)
                else:
                    both = mass[piece][:].bitcast(I32).unsqueeze(1).to_broadcast([P, 2, WIDTH])
                    nc.vector.scalar_tensor_tensor(shifted[:], both, -BIT_STEP, logits[piece, half][:], MULT, ADD)
                    nc.scalar.activation(e[piece][:, HALVES[half], :], shifted[:], EXP, bias=shift_bias[:], scale=SCALE)

        def attend(piece):
            sums[piece] = banks.tile([P, QUERY_BLOCKS, P + 1], F32, name=f"sums_{piece}", tag="bank")
            for b in range(KEY_BLOCKS):
                for c in range(QUERY_BLOCKS):
                    nc.tensor.matmul(
                        sums[piece][:, c, :],
                        e[piece][:, b, c * P : (c + 1) * P],
                        values[:, b, 0 : P + 1],
                        start=(b == 0 and c == 0),
                        stop=(b == KEY_BLOCKS - 1 and c == QUERY_BLOCKS - 1),
                    )

        for block in range(KEY_BLOCKS):
            for piece in EARLY:
                early_product(piece, block)
        late = [(piece, block) for piece in LATE for block in range(KEY_BLOCKS)]
        issued = 0
        for step in (largest_over_partitions, spread_tops):
            for early_piece, products in zip(EARLY, (2, 1)):
                for late_piece, block in late[issued : issued + products]:
                    late_product(late_piece, block)
                issued += products
                step(early_piece)
        tops_copy = held.tile([P, WIDTH], BF16, name="tops_copy")
        nc.vector.tensor_copy(tops_copy[:], tops[EARLY[1]][:])
        for late_piece, block in late[issued:]:
            late_product(late_piece, block)

        for early, late in zip(EARLY, LATE):
            flatten(late)
            exponentiate(early)
        for piece in LATE:
            weigh(piece)
            exponentiate(piece)
        for piece in range(PIECES):
            attend(piece)

        for piece in range(PIECES):
            inverse = held.tile([P, QUERY_BLOCKS, 1], F32, name=f"inverse_{piece}")
            nc.vector.reciprocal(inverse[:], sums[piece][:, :, ONES : ONES + 1])
            blocks_at_once = QUERY_BLOCKS if piece < PIECES - 1 else 1
            for c in range(0, QUERY_BLOCKS, blocks_at_once):
                these = slice(c, c + blocks_at_once)
                shape = [P, blocks_at_once, P]
                attended = held.tile(shape, F32, name=f"attended_{piece}_{c}")
                nc.vector.tensor_mul(attended[:], sums[piece][:, these, 0:P], inverse[:, these, :].to_broadcast(shape))
                flipped = banks.tile(shape, F32, name="flipped", tag="bank")
                for b in range(blocks_at_once):
                    nc.tensor.transpose(flipped[:, b, :], attended[:, b, :], identity[:])
                result = held.tile(shape, F32, name=f"result_{piece}_{c}")
                nc.scalar.copy(result[:], flipped[:])
                first = piece * WIDTH + c * P
                columns = out[:, first : first + blocks_at_once * P]
                nc.sync.dma_start(columns.rearrange("d (b i) -> d b i", b=blocks_at_once), result[:])
